import numpy as np
import ml_dtypes

BF16 = ml_dtypes.bfloat16


def bf(x):
    return np.asarray(x, np.float32).astype(BF16)


def f32(x):
    return np.asarray(x, np.float32)


def f64(x):
    return np.asarray(x).astype(np.float64)


def striped(idx):
    return np.tile(idx.reshape(-1, 16).T, (8, 1))


C, S, N = 256, 2048, 512


def setup_inputs():
    base = f32(np.random.standard_normal((C, S)))
    tok0 = f32(np.random.standard_normal((C, N)))
    tok1 = f32(np.random.standard_normal((C, N)))
    prev = f32(np.random.standard_normal((C, N)))
    ref = f32(np.tile(np.random.random((1, N)) < 0.5, (C, 1)))
    return {"base": base, "tok0": tok0, "tok1": tok1, "prev": prev, "ref": ref, "offs": striped(np.random.permutation(S)[:N])}


def reference(base, tok0, tok1, prev, ref, offs):
    idx = offs[:16].T.reshape(-1)
    m = f64(ref)
    res = f64(base).copy()
    res[:, idx] = m * f64(prev) + (1.0 - m) * (f64(tok0) + f64(tok1))
    return res

@@ -1,0 +1,46 @@
+import concourse.mybir as mybir
+
+F32 = mybir.dt.float32
+U16 = mybir.dt.uint16
+ADD = mybir.AluOpType.add
+MULT = mybir.AluOpType.mult
+
+P = 128
+
+
+def tile_fileencoder_kernel(tc, base, tok0, tok1, prev, ref, offs, out):
+    nc = tc.nc
+    channels, slots = base.shape
+    trees = tok0.shape[1]
+
+    with tc.tile_pool(name="held", bufs=1) as held, tc.tile_pool(name="work", bufs=2) as work:
+        offsets = held.tile([P, trees // 16], U16, name="offsets")
+        nc.sync.dma_start(offsets[:], offs)
+
+        for c0 in range(0, channels, P):
+            rows = slice(c0, c0 + P)
+
+            first = work.tile([P, trees], F32, name="first")
+            second = work.tile([P, trees], F32, name="second")
+            is_ref = work.tile([P, trees], F32, name="is_ref")
+            earlier = work.tile([P, trees], F32, name="earlier")
+            store = work.tile([P, slots], F32, name="store")
+            nc.sync.dma_start(first[:], tok0[rows, :])
+            nc.sync.dma_start(second[:], tok1[rows, :])
+            nc.sync.dma_start(is_ref[:], ref[rows, :])
+            nc.sync.dma_start(earlier[:], prev[rows, :])
+            nc.sync.dma_start(store[:], base[rows, :])
+
+            own = work.tile([P, trees], F32, name="own")
+            nc.vector.tensor_tensor(own[:], first[:], second[:], ADD)
+            not_ref = work.tile([P, trees], F32, name="not_ref")
+            nc.vector.tensor_scalar(not_ref[:], is_ref[:], -1.0, 1.0, MULT, ADD)
+            own_term = work.tile([P, trees], F32, name="own_term")
+            nc.vector.tensor_tensor(own_term[:], not_ref[:], own[:], MULT)
+
+            ref_term = work.tile([P, trees], F32, name="ref_term")
+            nc.vector.tensor_tensor(ref_term[:], is_ref[:], earlier[:], MULT)
+
+            nc.vector.tensor_tensor(store[:].indirect(offsets[:]), ref_term[:], own_term[:], ADD)
+
+            nc.sync.dma_start(out[rows, :], store[:])

@@ -4,6 +4,7 @@ F32 = mybir.dt.float32
 U16 = mybir.dt.uint16
 ADD = mybir.AluOpType.add
 MULT = mybir.AluOpType.mult
+COPY = mybir.ActivationFunctionType.Copy
 
 P = 128
 
@@ -34,7 +35,7 @@ def tile_fileencoder_kernel(tc, base, tok0, tok1, prev, ref, offs, out):
             own = work.tile([P, trees], F32, name="own")
             nc.vector.tensor_tensor(own[:], first[:], second[:], ADD)
             not_ref = work.tile([P, trees], F32, name="not_ref")
-            nc.vector.tensor_scalar(not_ref[:], is_ref[:], -1.0, 1.0, MULT, ADD)
+            nc.scalar.activation(not_ref[:], is_ref[:], COPY, bias=1.0, scale=-1.0)
             own_term = work.tile([P, trees], F32, name="own_term")
             nc.vector.tensor_tensor(own_term[:], not_ref[:], own[:], MULT)
 

@@ -18,24 +18,25 @@ def tile_fileencoder_kernel(tc, base, tok0, tok1, prev, ref, offs, out):
         offsets = held.tile([P, trees // 16], U16, name="offsets")
         nc.sync.dma_start(offsets[:], offs)
 
+        is_ref = held.tile([P, trees], F32, name="is_ref")
+        nc.sync.dma_start(is_ref[:], ref[0:P, :])
+        not_ref = held.tile([P, trees], F32, name="not_ref")
+        nc.scalar.activation(not_ref[:], is_ref[:], COPY, bias=1.0, scale=-1.0)
+
         for c0 in range(0, channels, P):
             rows = slice(c0, c0 + P)
 
             first = work.tile([P, trees], F32, name="first")
             second = work.tile([P, trees], F32, name="second")
-            is_ref = work.tile([P, trees], F32, name="is_ref")
             earlier = work.tile([P, trees], F32, name="earlier")
             store = work.tile([P, slots], F32, name="store")
             nc.sync.dma_start(first[:], tok0[rows, :])
             nc.sync.dma_start(second[:], tok1[rows, :])
-            nc.sync.dma_start(is_ref[:], ref[rows, :])
             nc.sync.dma_start(earlier[:], prev[rows, :])
             nc.sync.dma_start(store[:], base[rows, :])
 
             own = work.tile([P, trees], F32, name="own")
             nc.vector.tensor_tensor(own[:], first[:], second[:], ADD)
-            not_ref = work.tile([P, trees], F32, name="not_ref")
-            nc.scalar.activation(not_ref[:], is_ref[:], COPY, bias=1.0, scale=-1.0)
             own_term = work.tile([P, trees], F32, name="own_term")
             nc.vector.tensor_tensor(own_term[:], not_ref[:], own[:], MULT)
 

@@ -36,12 +36,12 @@ def tile_fileencoder_kernel(tc, base, tok0, tok1, prev, ref, offs, out):
             nc.sync.dma_start(store[:], base[rows, :])
 
             own = work.tile([P, trees], F32, name="own")
-            nc.vector.tensor_tensor(own[:], first[:], second[:], ADD)
+            nc.gpsimd.tensor_tensor(own[:], first[:], second[:], ADD)
             own_term = work.tile([P, trees], F32, name="own_term")
             nc.vector.tensor_tensor(own_term[:], not_ref[:], own[:], MULT)
 
             ref_term = work.tile([P, trees], F32, name="ref_term")
-            nc.vector.tensor_tensor(ref_term[:], is_ref[:], earlier[:], MULT)
+            nc.gpsimd.tensor_tensor(ref_term[:], is_ref[:], earlier[:], MULT)
 
             nc.vector.tensor_tensor(store[:].indirect(offsets[:]), ref_term[:], own_term[:], ADD)
 

@@ -13,36 +13,40 @@ def tile_fileencoder_kernel(tc, base, tok0, tok1, prev, ref, offs, out):
     nc = tc.nc
     channels, slots = base.shape
     trees = tok0.shape[1]
+    blocks = channels // P
 
-    with tc.tile_pool(name="held", bufs=1) as held, tc.tile_pool(name="work", bufs=2) as work:
+    with tc.tile_pool(name="held", bufs=1) as held:
         offsets = held.tile([P, trees // 16], U16, name="offsets")
         nc.sync.dma_start(offsets[:], offs)
 
         is_ref = held.tile([P, trees], F32, name="is_ref")
         nc.sync.dma_start(is_ref[:], ref[0:P, :])
+
+        first, second, earlier, store = [], [], [], []
+        for b in range(blocks):
+            rows = slice(b * P, (b + 1) * P)
+            first.append(held.tile([P, trees], F32, name=f"first{b}"))
+            second.append(held.tile([P, trees], F32, name=f"second{b}"))
+            earlier.append(held.tile([P, trees], F32, name=f"earlier{b}"))
+            nc.sync.dma_start(first[b][:], tok0[rows, :])
+            nc.sync.dma_start(second[b][:], tok1[rows, :])
+            nc.sync.dma_start(earlier[b][:], prev[rows, :])
+        for b in range(blocks):
+            store.append(held.tile([P, slots], F32, name=f"store{b}"))
+            nc.sync.dma_start(store[b][:], base[b * P : (b + 1) * P, :])
+
         not_ref = held.tile([P, trees], F32, name="not_ref")
         nc.scalar.activation(not_ref[:], is_ref[:], COPY, bias=1.0, scale=-1.0)
 
-        for c0 in range(0, channels, P):
-            rows = slice(c0, c0 + P)
+        own_term, ref_term = [], []
+        for b in range(blocks):
+            own = held.tile([P, trees], F32, name=f"own{b}")
+            nc.vector.tensor_tensor(own[:], first[b][:], second[b][:], ADD)
+            own_term.append(held.tile([P, trees], F32, name=f"own_term{b}"))
+            nc.vector.tensor_tensor(own_term[b][:], not_ref[:], own[:], MULT)
+            ref_term.append(held.tile([P, trees], F32, name=f"ref_term{b}"))
+            nc.vector.tensor_tensor(ref_term[b][:], is_ref[:], earlier[b][:], MULT)
 
-            first = work.tile([P, trees], F32, name="first")
-            second = work.tile([P, trees], F32, name="second")
-            earlier = work.tile([P, trees], F32, name="earlier")
-            store = work.tile([P, slots], F32, name="store")
-            nc.sync.dma_start(first[:], tok0[rows, :])
-            nc.sync.dma_start(second[:], tok1[rows, :])
-            nc.sync.dma_start(earlier[:], prev[rows, :])
-            nc.sync.dma_start(store[:], base[rows, :])
-
-            own = work.tile([P, trees], F32, name="own")
-            nc.gpsimd.tensor_tensor(own[:], first[:], second[:], ADD)
-            own_term = work.tile([P, trees], F32, name="own_term")
-            nc.vector.tensor_tensor(own_term[:], not_ref[:], own[:], MULT)
-
-            ref_term = work.tile([P, trees], F32, name="ref_term")
-            nc.gpsimd.tensor_tensor(ref_term[:], is_ref[:], earlier[:], MULT)
-
-            nc.vector.tensor_tensor(store[:].indirect(offsets[:]), ref_term[:], own_term[:], ADD)
-
-            nc.sync.dma_start(out[rows, :], store[:])
+        for b in range(blocks):
+            nc.vector.tensor_tensor(store[b][:].indirect(offsets[:]), ref_term[b][:], own_term[b][:], ADD)
+            nc.sync.dma_start(out[b * P : (b + 1) * P, :], store[b][:])

@@ -15,38 +15,39 @@ def tile_fileencoder_kernel(tc, base, tok0, tok1, prev, ref, offs, out):
     trees = tok0.shape[1]
     blocks = channels // P
 
+    ref_half = slice(0, trees)
+    own_half = slice(trees, 2 * trees)
+
     with tc.tile_pool(name="held", bufs=1) as held:
         offsets = held.tile([P, trees // 16], U16, name="offsets")
         nc.sync.dma_start(offsets[:], offs)
 
-        is_ref = held.tile([P, trees], F32, name="is_ref")
-        nc.sync.dma_start(is_ref[:], ref[0:P, :])
+        weights = held.tile([P, 2 * trees], F32, name="weights")
+        nc.sync.dma_start(weights[:, ref_half], ref[0:P, :])
 
-        first, second, earlier, store = [], [], [], []
+        first, second, values, store = [], [], [], []
         for b in range(blocks):
             rows = slice(b * P, (b + 1) * P)
             first.append(held.tile([P, trees], F32, name=f"first{b}"))
             second.append(held.tile([P, trees], F32, name=f"second{b}"))
-            earlier.append(held.tile([P, trees], F32, name=f"earlier{b}"))
+            values.append(held.tile([P, 2 * trees], F32, name=f"values{b}"))
             nc.sync.dma_start(first[b][:], tok0[rows, :])
             nc.sync.dma_start(second[b][:], tok1[rows, :])
-            nc.sync.dma_start(earlier[b][:], prev[rows, :])
+            nc.sync.dma_start(values[b][:, ref_half], prev[rows, :])
         for b in range(blocks):
             store.append(held.tile([P, slots], F32, name=f"store{b}"))
             nc.sync.dma_start(store[b][:], base[b * P : (b + 1) * P, :])
 
-        not_ref = held.tile([P, trees], F32, name="not_ref")
-        nc.scalar.activation(not_ref[:], is_ref[:], COPY, bias=1.0, scale=-1.0)
+        nc.scalar.activation(weights[:, own_half], weights[:, ref_half], COPY, bias=1.0, scale=-1.0)
 
-        own_term, ref_term = [], []
+        terms = []
         for b in range(blocks):
-            own = held.tile([P, trees], F32, name=f"own{b}")
-            nc.vector.tensor_tensor(own[:], first[b][:], second[b][:], ADD)
-            own_term.append(held.tile([P, trees], F32, name=f"own_term{b}"))
-            nc.vector.tensor_tensor(own_term[b][:], not_ref[:], own[:], MULT)
-            ref_term.append(held.tile([P, trees], F32, name=f"ref_term{b}"))
-            nc.vector.tensor_tensor(ref_term[b][:], is_ref[:], earlier[b][:], MULT)
+            nc.vector.tensor_tensor(values[b][:, own_half], first[b][:], second[b][:], ADD)
+            terms.append(held.tile([P, 2 * trees], F32, name=f"terms{b}"))
+            nc.vector.tensor_tensor(terms[b][:], weights[:], values[b][:], MULT)
 
         for b in range(blocks):
-            nc.vector.tensor_tensor(store[b][:].indirect(offsets[:]), ref_term[b][:], own_term[b][:], ADD)
+            nc.vector.tensor_tensor(
+                store[b][:].indirect(offsets[:]), terms[b][:, ref_half], terms[b][:, own_half], ADD
+            )
             nc.sync.dma_start(out[b * P : (b + 1) * P, :], store[b][:])

@@ -1,12 +1,14 @@
 import concourse.mybir as mybir
 
 F32 = mybir.dt.float32
+BF16 = mybir.dt.bfloat16
 U16 = mybir.dt.uint16
 ADD = mybir.AluOpType.add
 MULT = mybir.AluOpType.mult
 COPY = mybir.ActivationFunctionType.Copy
 
 P = 128
+REF_ROWS = 32
 
 
 def tile_fileencoder_kernel(tc, base, tok0, tok1, prev, ref, offs, out):
@@ -18,12 +20,14 @@ def tile_fileencoder_kernel(tc, base, tok0, tok1, prev, ref, offs, out):
     ref_half = slice(0, trees)
     own_half = slice(trees, 2 * trees)
 
-    with tc.tile_pool(name="held", bufs=1) as held:
+    with tc.tile_pool(name="held", bufs=1) as held, tc.psum_pool(name="spread", bufs=1) as spread:
         offsets = held.tile([P, trees // 16], U16, name="offsets")
         nc.sync.dma_start(offsets[:], offs)
 
-        weights = held.tile([P, 2 * trees], F32, name="weights")
-        nc.sync.dma_start(weights[:, ref_half], ref[0:P, :])
+        ref_rows = held.tile([REF_ROWS, trees], F32, name="ref_rows")
+        nc.sync.dma_start(ref_rows[:], ref[0:REF_ROWS, :])
+        share = held.tile([REF_ROWS, P], BF16, name="share")
+        nc.gpsimd.memset(share[:], 1.0 / REF_ROWS)
 
         first, second, values, store = [], [], [], []
         for b in range(blocks):
@@ -38,7 +42,11 @@ def tile_fileencoder_kernel(tc, base, tok0, tok1, prev, ref, offs, out):
             store.append(held.tile([P, slots], F32, name=f"store{b}"))
             nc.sync.dma_start(store[b][:], base[b * P : (b + 1) * P, :])
 
-        nc.scalar.activation(weights[:, own_half], weights[:, ref_half], COPY, bias=1.0, scale=-1.0)
+        ref_all = spread.tile([P, trees], F32, name="ref_all")
+        nc.tensor.matmul(ref_all[:], share[:], ref_rows[:].bitcast(BF16)[:, 1::2], start=True, stop=True)
+        weights = held.tile([P, 2 * trees], F32, name="weights")
+        nc.scalar.copy(weights[:, ref_half], ref_all[:])
+        nc.scalar.activation(weights[:, own_half], ref_all[:], COPY, bias=1.0, scale=-1.0)
 
         terms = []
         for b in range(blocks):

@@ -5,10 +5,9 @@ BF16 = mybir.dt.bfloat16
 U16 = mybir.dt.uint16
 ADD = mybir.AluOpType.add
 MULT = mybir.AluOpType.mult
-COPY = mybir.ActivationFunctionType.Copy
+IS_EQUAL = mybir.AluOpType.is_equal
 
 P = 128
-REF_ROWS = 32
 
 
 def tile_fileencoder_kernel(tc, base, tok0, tok1, prev, ref, offs, out):
@@ -17,45 +16,40 @@ def tile_fileencoder_kernel(tc, base, tok0, tok1, prev, ref, offs, out):
     trees = tok0.shape[1]
     blocks = channels // P
 
-    ref_half = slice(0, trees)
-    own_half = slice(trees, 2 * trees)
-
     with tc.tile_pool(name="held", bufs=1) as held, tc.psum_pool(name="spread", bufs=1) as spread:
         offsets = held.tile([P, trees // 16], U16, name="offsets")
         nc.sync.dma_start(offsets[:], offs)
 
-        ref_rows = held.tile([REF_ROWS, trees], F32, name="ref_rows")
-        nc.sync.dma_start(ref_rows[:], ref[0:REF_ROWS, :])
-        share = held.tile([REF_ROWS, P], BF16, name="share")
-        nc.gpsimd.memset(share[:], 1.0 / REF_ROWS)
+        ref_row = held.tile([1, trees], F32, name="ref_row")
+        nc.sync.dma_start(ref_row[:], ref[0:1, :])
+        ones = held.tile([1, P], BF16, name="ones")
+        nc.gpsimd.memset(ones[:], 1.0)
 
-        first, second, values, store = [], [], [], []
+        first, second, earlier, store = [], [], [], []
         for b in range(blocks):
             rows = slice(b * P, (b + 1) * P)
             first.append(held.tile([P, trees], F32, name=f"first{b}"))
             second.append(held.tile([P, trees], F32, name=f"second{b}"))
-            values.append(held.tile([P, 2 * trees], F32, name=f"values{b}"))
+            earlier.append(held.tile([P, trees], F32, name=f"earlier{b}"))
             nc.sync.dma_start(first[b][:], tok0[rows, :])
             nc.sync.dma_start(second[b][:], tok1[rows, :])
-            nc.sync.dma_start(values[b][:, ref_half], prev[rows, :])
+            nc.sync.dma_start(earlier[b][:], prev[rows, :])
         for b in range(blocks):
             store.append(held.tile([P, slots], F32, name=f"store{b}"))
             nc.sync.dma_start(store[b][:], base[b * P : (b + 1) * P, :])
 
         ref_all = spread.tile([P, trees], F32, name="ref_all")
-        nc.tensor.matmul(ref_all[:], share[:], ref_rows[:].bitcast(BF16)[:, 1::2], start=True, stop=True)
-        weights = held.tile([P, 2 * trees], F32, name="weights")
-        nc.scalar.copy(weights[:, ref_half], ref_all[:])
-        nc.scalar.activation(weights[:, own_half], ref_all[:], COPY, bias=1.0, scale=-1.0)
+        nc.tensor.matmul(ref_all[:], ones[:], ref_row[:].bitcast(BF16)[:, 1::2], start=True, stop=True)
 
-        terms = []
+        ref_term, own_term = [], []
         for b in range(blocks):
-            nc.vector.tensor_tensor(values[b][:, own_half], first[b][:], second[b][:], ADD)
-            terms.append(held.tile([P, 2 * trees], F32, name=f"terms{b}"))
-            nc.vector.tensor_tensor(terms[b][:], weights[:], values[b][:], MULT)
+            own = held.tile([P, trees], F32, name=f"own{b}")
+            ref_term.append(held.tile([P, trees], F32, name=f"ref_term{b}"))
+            own_term.append(held.tile([P, trees], F32, name=f"own_term{b}"))
+            nc.vector.tensor_tensor(own[:], first[b][:], second[b][:], ADD)
+            nc.vector.tensor_tensor(ref_term[b][:], ref_all[:], earlier[b][:], MULT)
+            nc.vector.scalar_tensor_tensor(own_term[b][:], ref_all[:], 0.0, own[:], IS_EQUAL, MULT)
 
         for b in range(blocks):
-            nc.vector.tensor_tensor(
-                store[b][:].indirect(offsets[:]), terms[b][:, ref_half], terms[b][:, own_half], ADD
-            )
+            nc.vector.tensor_tensor(store[b][:].indirect(offsets[:]), ref_term[b][:], own_term[b][:], ADD)
             nc.sync.dma_start(out[b * P : (b + 1) * P, :], store[b][:])

@@ -25,15 +25,17 @@ def tile_fileencoder_kernel(tc, base, tok0, tok1, prev, ref, offs, out):
         ones = held.tile([1, P], BF16, name="ones")
         nc.gpsimd.memset(ones[:], 1.0)
 
+        queues = [nc.sync, nc.scalar]
+        small_loads = []
         first, second, earlier, store = [], [], [], []
         for b in range(blocks):
             rows = slice(b * P, (b + 1) * P)
             first.append(held.tile([P, trees], F32, name=f"first{b}"))
             second.append(held.tile([P, trees], F32, name=f"second{b}"))
             earlier.append(held.tile([P, trees], F32, name=f"earlier{b}"))
-            nc.sync.dma_start(first[b][:], tok0[rows, :])
-            nc.sync.dma_start(second[b][:], tok1[rows, :])
-            nc.sync.dma_start(earlier[b][:], prev[rows, :])
+            small_loads.extend([(first[b], tok0[rows, :]), (second[b], tok1[rows, :]), (earlier[b], prev[rows, :])])
+        for turn, (tile, rows_in_dram) in enumerate(small_loads):
+            queues[turn % 2].dma_start(tile[:], rows_in_dram)
         for b in range(blocks):
             store.append(held.tile([P, slots], F32, name=f"store{b}"))
             nc.sync.dma_start(store[b][:], base[b * P : (b + 1) * P, :])

@@ -17,11 +17,8 @@ def tile_fileencoder_kernel(tc, base, tok0, tok1, prev, ref, offs, out):
     blocks = channels // P
 
     with tc.tile_pool(name="held", bufs=1) as held, tc.psum_pool(name="spread", bufs=1) as spread:
-        offsets = held.tile([P, trees // 16], U16, name="offsets")
-        nc.sync.dma_start(offsets[:], offs)
-
         ref_row = held.tile([1, trees], F32, name="ref_row")
-        nc.sync.dma_start(ref_row[:], ref[0:1, :])
+        nc.scalar.dma_start(ref_row[:], ref[0:1, :])
         ones = held.tile([1, P], BF16, name="ones")
         nc.gpsimd.memset(ones[:], 1.0)
 
@@ -36,6 +33,8 @@ def tile_fileencoder_kernel(tc, base, tok0, tok1, prev, ref, offs, out):
             small_loads.extend([(first[b], tok0[rows, :]), (second[b], tok1[rows, :]), (earlier[b], prev[rows, :])])
         for turn, (tile, rows_in_dram) in enumerate(small_loads):
             queues[turn % 2].dma_start(tile[:], rows_in_dram)
+        offsets = held.tile([P, trees // 16], U16, name="offsets")
+        nc.sync.dma_start(offsets[:], offs)
         for b in range(blocks):
             store.append(held.tile([P, slots], F32, name=f"store{b}"))
             nc.sync.dma_start(store[b][:], base[b * P : (b + 1) * P, :])

@@ -22,35 +22,33 @@ def tile_fileencoder_kernel(tc, base, tok0, tok1, prev, ref, offs, out):
         ones = held.tile([1, P], BF16, name="ones")
         nc.gpsimd.memset(ones[:], 1.0)
 
-        queues = [nc.sync, nc.scalar]
-        small_loads = []
+        offsets = held.tile([P, trees // 16], U16, name="offsets")
+
         first, second, earlier, store = [], [], [], []
         for b in range(blocks):
             rows = slice(b * P, (b + 1) * P)
             first.append(held.tile([P, trees], F32, name=f"first{b}"))
             second.append(held.tile([P, trees], F32, name=f"second{b}"))
             earlier.append(held.tile([P, trees], F32, name=f"earlier{b}"))
-            small_loads.extend([(first[b], tok0[rows, :]), (second[b], tok1[rows, :]), (earlier[b], prev[rows, :])])
-        for turn, (tile, rows_in_dram) in enumerate(small_loads):
-            queues[turn % 2].dma_start(tile[:], rows_in_dram)
-        offsets = held.tile([P, trees // 16], U16, name="offsets")
-        nc.sync.dma_start(offsets[:], offs)
-        for b in range(blocks):
             store.append(held.tile([P, slots], F32, name=f"store{b}"))
-            nc.sync.dma_start(store[b][:], base[b * P : (b + 1) * P, :])
+            nc.sync.dma_start(first[b][:], tok0[rows, :])
+            beside = nc.scalar if b == 0 else nc.sync
+            beside.dma_start(second[b][:], tok1[rows, :])
+            nc.sync.dma_start(earlier[b][:], prev[rows, :])
+            if b == 0:
+                nc.sync.dma_start(offsets[:], offs)
+            nc.sync.dma_start(store[b][:], base[rows, :])
 
         ref_all = spread.tile([P, trees], F32, name="ref_all")
         nc.tensor.matmul(ref_all[:], ones[:], ref_row[:].bitcast(BF16)[:, 1::2], start=True, stop=True)
 
-        ref_term, own_term = [], []
         for b in range(blocks):
+            rows = slice(b * P, (b + 1) * P)
             own = held.tile([P, trees], F32, name=f"own{b}")
-            ref_term.append(held.tile([P, trees], F32, name=f"ref_term{b}"))
-            own_term.append(held.tile([P, trees], F32, name=f"own_term{b}"))
+            ref_term = held.tile([P, trees], F32, name=f"ref_term{b}")
+            own_term = held.tile([P, trees], F32, name=f"own_term{b}")
             nc.vector.tensor_tensor(own[:], first[b][:], second[b][:], ADD)
-            nc.vector.tensor_tensor(ref_term[b][:], ref_all[:], earlier[b][:], MULT)
-            nc.vector.scalar_tensor_tensor(own_term[b][:], ref_all[:], 0.0, own[:], IS_EQUAL, MULT)
-
-        for b in range(blocks):
-            nc.vector.tensor_tensor(store[b][:].indirect(offsets[:]), ref_term[b][:], own_term[b][:], ADD)
-            nc.sync.dma_start(out[b * P : (b + 1) * P, :], store[b][:])
+            nc.vector.scalar_tensor_tensor(own_term[:], ref_all[:], 0.0, own[:], IS_EQUAL, MULT)
+            nc.vector.tensor_tensor(ref_term[:], ref_all[:], earlier[b][:], MULT)
+            nc.vector.tensor_tensor(store[b][:].indirect(offsets[:]), ref_term[:], own_term[:], ADD)
+            nc.sync.dma_start(out[rows, :], store[b][:])

@@ -1,4 +1,5 @@
 import concourse.mybir as mybir
+from concourse.masks import make_identity
 
 F32 = mybir.dt.float32
 BF16 = mybir.dt.bfloat16
@@ -21,6 +22,8 @@ def tile_fileencoder_kernel(tc, base, tok0, tok1, prev, ref, offs, out):
         nc.scalar.dma_start(ref_row[:], ref[0:1, :])
         ones = held.tile([1, P], BF16, name="ones")
         nc.gpsimd.memset(ones[:], 1.0)
+        identity = held.tile([P, P], F32, name="identity")
+        make_identity(nc, identity[:])
 
         offsets = held.tile([P, trees // 16], U16, name="offsets")
 
@@ -42,13 +45,29 @@ def tile_fileencoder_kernel(tc, base, tok0, tok1, prev, ref, offs, out):
         ref_all = spread.tile([P, trees], F32, name="ref_all")
         nc.tensor.matmul(ref_all[:], ones[:], ref_row[:].bitcast(BF16)[:, 1::2], start=True, stop=True)
 
-        for b in range(blocks):
-            rows = slice(b * P, (b + 1) * P)
-            own = held.tile([P, trees], F32, name=f"own{b}")
-            ref_term = held.tile([P, trees], F32, name=f"ref_term{b}")
-            own_term = held.tile([P, trees], F32, name=f"own_term{b}")
-            nc.vector.tensor_tensor(own[:], first[b][:], second[b][:], ADD)
-            nc.vector.scalar_tensor_tensor(own_term[:], ref_all[:], 0.0, own[:], IS_EQUAL, MULT)
-            nc.vector.tensor_tensor(ref_term[:], ref_all[:], earlier[b][:], MULT)
-            nc.vector.tensor_tensor(store[b][:].indirect(offsets[:]), ref_term[:], own_term[:], ADD)
-            nc.sync.dma_start(out[rows, :], store[b][:])
+        ref_copy = held.tile([P, trees], F32, name="ref_copy")
+        nc.vector.tensor_copy(ref_copy[:], ref_all[:])
+
+        ref_term = [held.tile([P, trees], F32, name=f"ref_term{b}") for b in range(blocks)]
+        own_term = [held.tile([P, trees], F32, name=f"own_term{b}") for b in range(blocks)]
+        own = held.tile([P, trees], F32, name="own")
+        nc.vector.tensor_tensor(own[:], first[0][:], second[0][:], ADD)
+        nc.vector.tensor_tensor(ref_term[0][:], ref_all[:], earlier[0][:], MULT)
+        nc.vector.scalar_tensor_tensor(own_term[0][:], ref_all[:], 0.0, own[:], IS_EQUAL, MULT)
+
+        nc.vector.tensor_tensor(store[0][:].indirect(offsets[:]), ref_term[0][:], own_term[0][:], ADD)
+        nc.sync.dma_start(out[0:P, :], store[0][:])
+
+        half = trees // 2
+        halves = [slice(h * half, (h + 1) * half) for h in range(2)]
+        sums = [spread.tile([P, trees], F32, name=f"sums{h}") for h in range(2)]
+        for h, columns in enumerate(halves):
+            nc.tensor.matmul(sums[h][:, 0:half], identity[:], first[1][:, columns], start=True, stop=False)
+            nc.tensor.matmul(sums[h][:, 0:half], identity[:], second[1][:, columns], start=False, stop=True)
+        nc.vector.tensor_tensor(ref_term[1][:], ref_all[:], earlier[1][:], MULT)
+        for h, columns in enumerate(halves):
+            nc.vector.scalar_tensor_tensor(
+                own_term[1][:, columns], ref_copy[:, columns], 0.0, sums[h][:, 0:half], IS_EQUAL, MULT
+            )
+        nc.vector.tensor_tensor(store[1][:].indirect(offsets[:]), ref_term[1][:], own_term[1][:], ADD)
+        nc.sync.dma_start(out[P : 2 * P, :], store[1][:])

@@ -59,15 +59,14 @@ def tile_fileencoder_kernel(tc, base, tok0, tok1, prev, ref, offs, out):
         nc.sync.dma_start(out[0:P, :], store[0][:])
 
         half = trees // 2
-        halves = [slice(h * half, (h + 1) * half) for h in range(2)]
-        sums = [spread.tile([P, trees], F32, name=f"sums{h}") for h in range(2)]
-        for h, columns in enumerate(halves):
-            nc.tensor.matmul(sums[h][:, 0:half], identity[:], first[1][:, columns], start=True, stop=False)
-            nc.tensor.matmul(sums[h][:, 0:half], identity[:], second[1][:, columns], start=False, stop=True)
+        early, late = slice(0, half), slice(half, trees)
+        early_sums = spread.tile([P, half], F32, name="early_sums")
+        nc.tensor.matmul(early_sums[:], identity[:], first[1][:, early], start=True, stop=False)
+        nc.tensor.matmul(early_sums[:], identity[:], second[1][:, early], start=False, stop=True)
+        late_sums = held.tile([P, half], F32, name="late_sums")
+        nc.gpsimd.tensor_tensor(late_sums[:], first[1][:, late], second[1][:, late], ADD)
         nc.vector.tensor_tensor(ref_term[1][:], ref_all[:], earlier[1][:], MULT)
-        for h, columns in enumerate(halves):
-            nc.vector.scalar_tensor_tensor(
-                own_term[1][:, columns], ref_copy[:, columns], 0.0, sums[h][:, 0:half], IS_EQUAL, MULT
-            )
+        nc.vector.scalar_tensor_tensor(own_term[1][:, early], ref_copy[:, early], 0.0, early_sums[:], IS_EQUAL, MULT)
+        nc.vector.scalar_tensor_tensor(own_term[1][:, late], ref_all[:, late], 0.0, late_sums[:], IS_EQUAL, MULT)
         nc.vector.tensor_tensor(store[1][:].indirect(offsets[:]), ref_term[1][:], own_term[1][:], ADD)
         nc.sync.dma_start(out[P : 2 * P, :], store[1][:])

import concourse.mybir as mybir
from concourse.masks import make_identity

F32 = mybir.dt.float32
BF16 = mybir.dt.bfloat16
U16 = mybir.dt.uint16
ADD = mybir.AluOpType.add
MULT = mybir.AluOpType.mult
IS_EQUAL = mybir.AluOpType.is_equal

P = 128


def tile_fileencoder_kernel(tc, base, tok0, tok1, prev, ref, offs, out):
    nc = tc.nc
    channels, slots = base.shape
    trees = tok0.shape[1]
    blocks = channels // P

    with tc.tile_pool(name="held", bufs=1) as held, tc.psum_pool(name="spread", bufs=1) as spread:
        ref_row = held.tile([1, trees], F32, name="ref_row")
        nc.scalar.dma_start(ref_row[:], ref[0:1, :])
        ones = held.tile([1, P], BF16, name="ones")
        nc.gpsimd.memset(ones[:], 1.0)
        identity = held.tile([P, P], F32, name="identity")
        make_identity(nc, identity[:])

        offsets = held.tile([P, trees // 16], U16, name="offsets")

        first, second, earlier, store = [], [], [], []
        for b in range(blocks):
            rows = slice(b * P, (b + 1) * P)
            first.append(held.tile([P, trees], F32, name=f"first{b}"))
            second.append(held.tile([P, trees], F32, name=f"second{b}"))
            earlier.append(held.tile([P, trees], F32, name=f"earlier{b}"))
            store.append(held.tile([P, slots], F32, name=f"store{b}"))
            nc.sync.dma_start(first[b][:], tok0[rows, :])
            beside = nc.scalar if b == 0 else nc.sync
            beside.dma_start(second[b][:], tok1[rows, :])
            nc.sync.dma_start(earlier[b][:], prev[rows, :])
            if b == 0:
                nc.sync.dma_start(offsets[:], offs)
            nc.sync.dma_start(store[b][:], base[rows, :])

        ref_all = spread.tile([P, trees], F32, name="ref_all")
        nc.tensor.matmul(ref_all[:], ones[:], ref_row[:].bitcast(BF16)[:, 1::2], start=True, stop=True)

        ref_copy = held.tile([P, trees], F32, name="ref_copy")
        nc.vector.tensor_copy(ref_copy[:], ref_all[:])

        ref_term = [held.tile([P, trees], F32, name=f"ref_term{b}") for b in range(blocks)]
        own_term = [held.tile([P, trees], F32, name=f"own_term{b}") for b in range(blocks)]
        own = held.tile([P, trees], F32, name="own")
        nc.vector.tensor_tensor(own[:], first[0][:], second[0][:], ADD)
        nc.vector.tensor_tensor(ref_term[0][:], ref_all[:], earlier[0][:], MULT)
        nc.vector.scalar_tensor_tensor(own_term[0][:], ref_all[:], 0.0, own[:], IS_EQUAL, MULT)

        nc.vector.tensor_tensor(store[0][:].indirect(offsets[:]), ref_term[0][:], own_term[0][:], ADD)
        nc.sync.dma_start(out[0:P, :], store[0][:])

        half = trees // 2
        early, late = slice(0, half), slice(half, trees)
        early_sums = spread.tile([P, half], F32, name="early_sums")
        nc.tensor.matmul(early_sums[:], identity[:], first[1][:, early], start=True, stop=False)
        nc.tensor.matmul(early_sums[:], identity[:], second[1][:, early], start=False, stop=True)
        late_sums = held.tile([P, half], F32, name="late_sums")
        nc.gpsimd.tensor_tensor(late_sums[:], first[1][:, late], second[1][:, late], ADD)
        nc.vector.tensor_tensor(ref_term[1][:], ref_all[:], earlier[1][:], MULT)
        nc.vector.scalar_tensor_tensor(own_term[1][:, early], ref_copy[:, early], 0.0, early_sums[:], IS_EQUAL, MULT)
        nc.vector.scalar_tensor_tensor(own_term[1][:, late], ref_all[:, late], 0.0, late_sums[:], IS_EQUAL, MULT)
        nc.vector.tensor_tensor(store[1][:].indirect(offsets[:]), ref_term[1][:], own_term[1][:], ADD)
        nc.sync.dma_start(out[P : 2 * P, :], store[1][:])
